import numpy as np
import ml_dtypes


def mxq(x, axis, fmt="e4m3"):
    dtype, down = {"e4m3": (ml_dtypes.float8_e4m3fn, 7), "e5m2": (ml_dtypes.float8_e5m2, 14)}[fmt]
    v = np.moveaxis(np.asarray(x, np.float32).astype(ml_dtypes.bfloat16).astype(np.float64), axis, -1)
    blocks = v.reshape(v.shape[:-1] + (-1, 32))
    amax = np.abs(blocks).max(-1, keepdims=True)
    byte = np.maximum(np.where(amax > 0, np.frexp(amax)[1] - 1 + 127, 0) - down, 1)
    scale = np.exp2(byte - 127.0)
    codes = (blocks / scale).astype(np.float32).astype(dtype).astype(np.float64)
    return np.moveaxis((codes * scale).reshape(v.shape), -1, axis)


WIDE = False


def mx_kscale(k):
    if not WIDE:
        return np.ones(k)
    levels = np.array([10, -10, 5, -5, 0])
    a = np.random.permutation(np.resize(levels, k // 512 * 4)).reshape(k // 512, 4)
    idx = np.arange(k)
    return np.exp2(a[idx // 512, idx % 128 // 32])


BF16 = ml_dtypes.bfloat16


def bf(x):
    return np.asarray(x, np.float32).astype(BF16)


def f64(x):
    return np.asarray(x).astype(np.float64)


BS, CIN, COUT, OUT_DIM, BLK = 128, 4096, 128, 4, 4
D = OUT_DIM * BLK
K = CIN * BLK


def setup_inputs():
    s = mx_kscale(K)
    sd = np.tile(s.reshape(CIN, 1, BLK), (1, OUT_DIM, 1)).reshape(CIN, D)
    return {"x": bf(np.random.standard_normal((BS, CIN, D)) * sd),
            "weight": bf(np.random.standard_normal((COUT, CIN, D)) / sd)}


def reference(x, weight):
    bs, cin, d = x.shape
    cout = weight.shape[0]
    n = d // BLK
    xr = f64(x).reshape(bs, cin, n, BLK).transpose(2, 0, 1, 3).reshape(n, bs, cin * BLK)
    wr = f64(weight).reshape(cout, cin, n, BLK).transpose(2, 1, 3, 0).reshape(n, cin * BLK, cout)
    out = mxq(xr, 2, "e4m3") @ mxq(wr, 1, "e4m3")
    return out.transpose(1, 2, 0) / np.sqrt(cin)

import math
from contextlib import ExitStack

import concourse.mybir as mybir
from concourse.masks import make_identity

F32 = mybir.dt.float32
BF16 = mybir.dt.bfloat16
U32 = mybir.dt.uint32
U8 = mybir.dt.uint8
FP8X4 = mybir.dt.float8_e4m3fn_x4

P = 128
C_IN = 4096
POSITIONS = 4
WINDOW = 4
SIGNAL = POSITIONS * WINDOW
WORDS = SIGNAL // 2
PAIRS = WINDOW // 2
CHUNK = P
CHUNKS = C_IN // CHUNK
BANK_WORDS = 4
BANK_POSITIONS = BANK_WORDS // PAIRS
BANKS = WORDS // BANK_WORDS
BANK_COLUMNS = BANK_POSITIONS * P
CHUNKS_PER_ROUND = 1
ROUNDS = CHUNKS // CHUNKS_PER_ROUND
LOAD_BUFS = 8

FLOPS = 2 * P * P * C_IN * SIGNAL


def quantise(nc, grouped, codes, scales):
    nc.vector.quantize_mx(out=codes.bitcast(FP8X4), scales=scales, in_=grouped)


def multiply(nc, sums, chunk, operands):
    x_codes, x_scales, w_codes, w_scales = operands
    for n in range(POSITIONS):
        cols = slice(n * P, (n + 1) * P)
        nc.tensor.matmul_mx(
            out=sums[n],
            lhsT=x_codes[:, cols].bitcast(FP8X4),
            lhsT_scale=x_scales[:, cols],
            rhs=w_codes[:, cols].bitcast(FP8X4),
            rhs_scale=w_scales[:, cols],
            start=(chunk == 0),
            stop=(chunk == CHUNKS - 1),
        )


def tile_nonoverlappinglocallyconnected1d_k_kernel(tc, x, weight, out):
    nc = tc.nc
    with ExitStack() as ctx:
        const = ctx.enter_context(tc.tile_pool(name="const", bufs=1))
        loads = ctx.enter_context(tc.tile_pool(name="loads", bufs=LOAD_BUFS))
        stage = ctx.enter_context(tc.tile_pool(name="stage", bufs=4))
        packed = ctx.enter_context(tc.tile_pool(name="packed", bufs=2 * CHUNKS_PER_ROUND + 1))
        sum_banks = ctx.enter_context(tc.psum_pool(name="sum_banks", bufs=1))
        turn_banks = ctx.enter_context(tc.psum_pool(name="turn_banks", bufs=4))

        identity = const.tile([P, P], F32)
        make_identity(nc, identity[:])
        sums = [sum_banks.tile([P, P], F32, name="sum%d" % n)[:] for n in range(POSITIONS)]

        ctx.enter_context(tc.manual_schedule())

        unquantised = None
        earlier = []
        for r in range(ROUNDS):
            fresh = []
            for chunk in range(r * CHUNKS_PER_ROUND, (r + 1) * CHUNKS_PER_ROUND):
                channels = slice(chunk * CHUNK, (chunk + 1) * CHUNK)
                operands = []
                for label, source in (("x", x), ("w", weight)):
                    raw = loads.tile([P, CHUNK * SIGNAL], BF16, tag="raw_" + label)
                    nc.sync.dma_start(out=raw[:], in_=source[:, channels, :].rearrange("r i d -> r (i d)"))
                    words = raw[:].bitcast(F32).rearrange("r (i w) -> r i w", w=WORDS)
                    codes = packed.tile([P, POSITIONS * P], U32, tag="codes_" + label, align_bytes=64)
                    scales = packed.tile([P, POSITIONS * P], U8, tag="scales_" + label, align_bytes=64)
                    operands.extend([codes, scales])
                    for bank in range(BANKS):
                        turned = turn_banks.tile([P, BANK_WORDS, P], F32)
                        for j in range(BANK_WORDS):
                            nc.tensor.transpose(turned[:, j, :], words[:, :, bank * BANK_WORDS + j], identity[:])
                        grouped = stage.tile([P, BANK_COLUMNS * WINDOW], BF16, align_bytes=64)
                        grouped_words = grouped[:].bitcast(F32).rearrange(
                            "p (n r u) -> p n r u", n=BANK_POSITIONS, u=PAIRS
                        )
                        turned_words = turned[:].rearrange("p (n u) r -> p n r u", u=PAIRS)
                        if label == "w" and bank == BANKS - 1:
                            nc.vector.tensor_copy(out=grouped_words, in_=turned_words)
                        else:
                            nc.scalar.copy(out=grouped_words, in_=turned_words)
                        if unquantised is not None:
                            quantise(nc, *unquantised)
                        cols = slice(bank * BANK_COLUMNS, (bank + 1) * BANK_COLUMNS)
                        unquantised = (grouped[:], codes[:, cols], scales[:, cols])
                fresh.append((chunk, operands))
            for chunk, operands in earlier:
                multiply(nc, sums, chunk, operands)
            earlier = fresh
        quantise(nc, *unquantised)
        for chunk, operands in earlier:
            multiply(nc, sums, chunk, operands)

        planes = const.tile([P, POSITIONS, P], F32)
        for n in range(POSITIONS):
            if n % 2 == 0:
                nc.vector.tensor_copy(out=planes[:, n, :], in_=sums[n])
            else:
                nc.scalar.copy(out=planes[:, n, :], in_=sums[n])
        result = const.tile([P, P, POSITIONS], F32)
        nc.vector.tensor_scalar_mul(
            out=result[:], in0=planes[:].rearrange("b n o -> b o n"), scalar1=1.0 / math.sqrt(C_IN)
        )
        nc.sync.dma_start(out=out.rearrange("b o n -> b (o n)"), in_=result[:].rearrange("b o n -> b (o n)"))
